import numpy as np
import ml_dtypes


def mxq(x, axis, fmt="e4m3"):
    dtype, down = {"e4m3": (ml_dtypes.float8_e4m3fn, 7), "e5m2": (ml_dtypes.float8_e5m2, 14)}[fmt]
    v = np.moveaxis(np.asarray(x, np.float32).astype(ml_dtypes.bfloat16).astype(np.float64), axis, -1)
    blocks = v.reshape(v.shape[:-1] + (-1, 32))
    amax = np.abs(blocks).max(-1, keepdims=True)
    byte = np.maximum(np.where(amax > 0, np.frexp(amax)[1] - 1 + 127, 0) - down, 1)
    scale = np.exp2(byte - 127.0)
    codes = (blocks / scale).astype(np.float32).astype(dtype).astype(np.float64)
    return np.moveaxis((codes * scale).reshape(v.shape), -1, axis)


WIDE = False


def mx_kscale(k):
    if not WIDE:
        return np.ones(k)
    levels = np.array([10, -10, 5, -5, 0])
    if k % 512:
        return np.exp2(np.random.permutation(np.resize(levels, k // 32))).repeat(32)
    a = np.empty((k // 512, 16))
    for p in range(k // 512):
        a[p, :8] = np.random.permutation(np.resize(levels, 8))
        for g in range(8):
            far = levels[np.abs(levels - a[p, g]) >= 10]
            a[p, g + 8] = far[np.random.randint(len(far))]
    return np.exp2(a.ravel()).repeat(32)


BF16 = ml_dtypes.bfloat16


def bf(x):
    return np.asarray(x, np.float32).astype(BF16)


def f64(x):
    return np.asarray(x).astype(np.float64)


B, S, E, H, DH, L = 2, 512, 2048, 16, 128, 512
NOPE = DH // 4
ROPE_D = DH - NOPE
THETA = 10000.0


def rope_tables(seq_len):
    freqs = 1.0 / THETA ** (np.arange(0, ROPE_D, 2) / ROPE_D)
    emb = np.arange(seq_len)[:, None] * freqs[None, :]
    return np.cos(emb), np.sin(emb)


def apply_rope(x, cos, sin):
    xe, xo = x[..., ::2], x[..., 1::2]
    return np.concatenate([xe * cos - xo * sin, xo * cos + xe * sin], axis=-1)


def draw0():
    s, t = mx_kscale(E), mx_kscale(L)
    return {"x": bf(np.random.standard_normal((B, S, E)) * s),
            "Wkv_down": bf(np.random.standard_normal((E, L)) / np.sqrt(E) / s[:, None] * t),
            "Wk_up": bf(np.random.standard_normal((L, H * DH)) / np.sqrt(L) / t[:, None]),
            "Wv_up": bf(np.random.standard_normal((L, H * DH)) / np.sqrt(L) / t[:, None])}


def core(x, Wkv_down, Wk_up, Wv_up):
    c_kv = mxq(f64(x), 2, "e4m3") @ mxq(f64(Wkv_down), 0, "e4m3")
    cq = mxq(c_kv, 2, "e4m3")
    k = (cq @ mxq(f64(Wk_up), 0, "e4m3")).reshape(B, S, H, DH).transpose(0, 2, 1, 3)
    v = (cq @ mxq(f64(Wv_up), 0, "e4m3")).reshape(B, S, H, DH).transpose(0, 2, 1, 3)
    k_nope, k_rope = k[..., :NOPE], k[..., NOPE:]
    cos, sin = rope_tables(S)
    k_rope = apply_rope(k_rope, cos, sin)
    kf = np.concatenate([k_nope, k_rope], axis=-1)
    return kf, v


def e4m3fn_bytes(y):
    return np.clip(np.asarray(y, np.float64), -448.0, 448.0).astype(np.float32).astype(ml_dtypes.float8_e4m3fn).view(np.uint8)


def e4m3fn_values(b):
    return np.asarray(b, np.uint8).view(ml_dtypes.float8_e4m3fn).astype(np.float64)


def setup_inputs():
    d = draw0()
    x0 = np.asarray(d['x']).astype(np.float64)
    s = (np.max(np.abs(x0), axis=(0, 1), keepdims=True) / 448.0).astype(np.float32)
    out = {}
    for k, v in d.items():
        if k == 'x':
            out['x_bytes'] = e4m3fn_bytes(x0 / s.astype(np.float64))
            out['x_scale'] = s
        else:
            out[k] = v
    return out


def reference(x_bytes, x_scale, Wkv_down, Wk_up, Wv_up):
    return core(e4m3fn_values(x_bytes) * x_scale.astype(np.float64), Wkv_down, Wk_up, Wv_up)

from contextlib import ExitStack
import math

import concourse.mybir as mybir
from concourse.masks import make_identity

B, S, E, H, DH, L = 2, 512, 2048, 16, 128, 512
NOPE = DH // 4
ROPE = DH - NOPE
HALF = ROPE // 2
THETA = 10000.0

P = 128
PACK = 4
GROUPS = E // (P * PACK)
TILES = S // P
HG = 4
NHG = H // HG
OUT_BUFS = 10
FLOPS = 2 * B * S * E * L + 2 * 2 * B * S * L * H * DH

F32 = mybir.dt.float32
BF16 = mybir.dt.bfloat16
I32 = mybir.dt.int32
U32 = mybir.dt.uint32
U8 = mybir.dt.uint8
FP8 = mybir.dt.float8_e4m3fn
FP8X4 = mybir.dt.float8_e4m3fn_x4
MULT = mybir.AluOpType.mult
ADD = mybir.AluOpType.add
SUB = mybir.AluOpType.subtract
SIN = mybir.ActivationFunctionType.Sin


def tile_mla_pa_kernel(tc, x_bytes, x_scale, Wkv_down, Wk_up, Wv_up, out_0, out_1):
    nc = tc.nc
    with ExitStack() as ctx:
        const = ctx.enter_context(tc.tile_pool(name="const", bufs=1))
        keep = ctx.enter_context(tc.tile_pool(name="keep", bufs=1))
        work = ctx.enter_context(tc.tile_pool(name="work", bufs=3))
        outs = ctx.enter_context(tc.tile_pool(name="outs", bufs=OUT_BUFS))
        psum = ctx.enter_context(tc.psum_pool(name="psum", bufs=2))

        wd_raw = {}
        xb = {}
        w_raw = {}
        wd_view = Wkv_down.rearrange("(g p j) n -> g p j n", p=P, j=PACK)
        x_view = x_bytes.rearrange("b (q t) k -> b q t k", t=TILES)

        def load_wd(g):
            wd_raw[g] = keep.tile([P, PACK, L], BF16, name="wd_raw%d" % g)
            nc.sync.dma_start(out=wd_raw[g][:], in_=wd_view[g])

        def load_x(b, u):
            xb[(b, u)] = keep.tile([P, 2, E], U8, name="xb_%d_%d" % (b, u))
            nc.sync.dma_start(out=xb[(b, u)][:], in_=x_view[b, :, 2 * u : 2 * u + 2, :])

        def load_w(src, key, half):
            w_raw[(key, half)] = outs.tile([P, PACK, 1024], BF16, name="w_raw_%s%d" % (key, half), tag="o")
            nc.sync.dma_start(out=w_raw[(key, half)][:], in_=src.rearrange("(p j) n -> p j n", j=PACK)[:, :, 1024 * half : 1024 * half + 1024])

        scale_rows = const.tile([P, P], F32, name="scale_rows")
        nc.gpsimd.memset(scale_rows[:], 0.0)
        nc.sync.dma_start(out=scale_rows[0 : E // P, :], in_=x_scale.rearrange("a b (m n) -> (a b m) n", n=P))
        load_wd(0)
        load_x(0, 0)
        for g in range(1, GROUPS):
            load_wd(g)
        load_x(0, 1)
        load_w(Wv_up, "v", 0)
        load_w(Wv_up, "v", 1)
        load_w(Wk_up, "k", 0)
        load_w(Wk_up, "k", 1)
        load_x(1, 0)
        load_x(1, 1)

        ident = const.tile([P, P], F32, name="ident")
        make_identity(nc, ident[:])
        ident_bf = const.tile([P, P], BF16, name="ident_bf")
        make_identity(nc, ident_bf[:])
        warm = const.tile([P, 1], F32, name="warm")
        nc.gpsimd.memset(warm[:], 0.0)
        nc.scalar.activation(warm[:], warm[:], SIN)

        scale_bc = const.tile([P, E], F32, name="scale_bc")
        scale_cols = const.tile([P, E // P], F32, name="scale_cols")
        sp = psum.tile([P, P], F32, name="sp", tag="ps", bufs=4)
        nc.tensor.transpose(sp[:], scale_rows[:], ident[:])
        nc.scalar.copy(scale_cols[:], sp[:, 0 : E // P])
        for i in range(4):
            sp = psum.tile([P, 4, P], F32, name="sp", tag="ps", bufs=4)
            for m in range(4):
                nc.tensor.transpose(sp[:, m, :], scale_cols[:, 4 * i + m : 4 * i + m + 1].to_broadcast([P, P]), ident[:])
            eng = nc.scalar.copy if i % 2 else nc.vector.tensor_copy
            eng(scale_bc[:, 512 * i : 512 * i + 512], sp[:].rearrange("p m n -> p (m n)"))

        pos = const.tile([P, TILES], F32, name="pos")
        nc.gpsimd.iota(pos[:], pattern=[[1, TILES]], base=0, channel_multiplier=TILES, allow_small_or_imprecise_dtypes=True)
        turns = const.tile([P, 2, TILES, HALF], F32, name="turns")
        nc.gpsimd.tensor_scalar(turns[:, 0, :, 0], pos[:], 1.0 / (2.0 * math.pi), None, op0=MULT)
        done = 1
        while done < HALF:
            n = min(done, HALF - done)
            nc.gpsimd.tensor_scalar(turns[:, 0, :, done : done + n], turns[:, 0, :, 0:n], THETA ** (-2.0 * done / ROPE), 0.0, op0=MULT, op1=ADD)
            done += n
        nc.gpsimd.tensor_scalar(turns[:, 1], turns[:, 0], 1.0, 0.25, op0=MULT, op1=ADD)
        whole_i = const.tile([P, 2, TILES, HALF], I32, name="whole_i")
        whole = const.tile([P, 2, TILES, HALF], F32, name="whole")
        frac = const.tile([P, 2, TILES, HALF], F32, name="frac")
        trig = const.tile([P, 2, TILES, HALF], F32, name="trig")
        sin_tab = const.tile([P, TILES, 2, HALF], F32, name="sin_tab")

        def tables():
            nc.vector.tensor_copy(whole_i[:], turns[:])
            nc.vector.tensor_copy(whole[:], whole_i[:])
            nc.gpsimd.tensor_tensor(frac[:], turns[:], whole[:], op=SUB)
            nc.scalar.activation(sin_tab[:, :, 0, :], frac[:, 0], SIN, scale=-2.0 * math.pi)
            nc.scalar.activation(sin_tab[:, :, 1, :], frac[:, 0], SIN, scale=2.0 * math.pi)
            nc.scalar.activation(trig[:, 1], frac[:, 1], SIN, scale=2.0 * math.pi)

        def interleave(how, dst, src):
            if how == "S":
                nc.scalar.copy(dst, src)
            elif how == "V":
                nc.vector.tensor_copy(dst, src)

        def pe_pass(bank, lo, n, src):
            nc.tensor.matmul(bank[:, lo : lo + n], lhsT=ident_bf[:], rhs=src, start=True, stop=True)

        wd_q = keep.tile([P, GROUPS, L], U32, name="wd_q", align_bytes=64)
        wd_s = keep.tile([P, GROUPS, L], U8, name="wd_s", align_bytes=64)
        wv_q = keep.tile([P, H * DH], U32, name="wv_q", align_bytes=64)
        wv_s = keep.tile([P, H * DH], U8, name="wv_s", align_bytes=64)
        wn_q = keep.tile([P, H * NOPE], U32, name="wn_q", align_bytes=64)
        wn_s = keep.tile([P, H * NOPE], U8, name="wn_s", align_bytes=64)
        wr_q = keep.tile([P, H * ROPE], U32, name="wr_q", align_bytes=64)
        wr_s = keep.tile([P, H * ROPE], U8, name="wr_s", align_bytes=64)
        grp = {}

        def group_tile(key):
            grp[key] = work.tile([P, L * PACK], BF16, name="grouped", bufs=4, align_bytes=64)
            return grp[key]

        def interleave_bank(dst, srcs):
            total = sum(n for n, view in srcs)
            bank = psum.tile([P, 1024], BF16, name="bank", tag="ps", bufs=4)
            lo = 0
            for n, view in srcs:
                nc.tensor.matmul(bank[:, lo : lo + n], lhsT=ident_bf[:], rhs=view, start=True, stop=True)
                lo += n
            nc.scalar.copy(dst, bank[:, 0:total])

        def wd_int(g, how):
            grouped = group_tile(("d", g))
            src = wd_raw[g][:].rearrange("p j (m t) -> p t m j", t=PACK)
            if how == "P":
                for i in range(2):
                    interleave_bank(grouped[:, 1024 * i : 1024 * i + 1024], [(512, src[:, 2 * i]), (512, src[:, 2 * i + 1])])
            else:
                interleave(how, grouped[:].rearrange("p (t m j) -> p t m j", t=PACK, j=PACK), src)

        def wd_quant(g):
            nc.vector.quantize_mx(out=wd_q[:, g, :].bitcast(FP8X4), scales=wd_s[:, g, :], in_=grp[("d", g)][:])

        def wv_int(c, how):
            grouped = group_tile(("v", c))
            src = w_raw[("v", c // 2)][:, :, 512 * (c % 2) : 512 * (c % 2) + 512].rearrange("p j n -> p n j")
            if how == "P":
                for i in range(2):
                    interleave_bank(grouped[:, 1024 * i : 1024 * i + 1024],
                                    [(512, src[:, 256 * i : 256 * i + 128]), (512, src[:, 256 * i + 128 : 256 * i + 256])])
            else:
                interleave(how, grouped[:].rearrange("p (n j) -> p n j", j=PACK), src)

        def wv_quant(c):
            cols = slice(512 * c, 512 * c + 512)
            nc.vector.quantize_mx(out=wv_q[:, cols].bitcast(FP8X4), scales=wv_s[:, cols], in_=grp[("v", c)][:])

        def wn_int(how):
            grouped = group_tile("n")
            for half in range(2):
                src = w_raw[("k", half)][:].rearrange("p j (h f) -> p h f j", f=DH)[:, :, 0:NOPE, :]
                if how == "P":
                    interleave_bank(grouped[:, 1024 * half : 1024 * half + 1024], [(512, src[:, 0:4]), (512, src[:, 4:8])])
                else:
                    interleave(how, grouped[:, 1024 * half : 1024 * half + 1024].rearrange("p (h f j) -> p h f j", f=NOPE, j=PACK), src)

        def wn_quant():
            nc.vector.quantize_mx(out=wn_q[:].bitcast(FP8X4), scales=wn_s[:], in_=grp["n"][:])

        RC = HG * ROPE * PACK

        def wr_int(c, how):
            half, e = c // 2, c % 2
            if e == 0:
                grp[("r", half)] = work.tile([P, 2 * RC], BF16, name="grouped_r", bufs=2, align_bytes=64)
            grouped = grp[("r", half)][:, RC * e : RC * e + RC]
            src = w_raw[("k", half)][:].rearrange("p j (h f) -> p h f j", f=DH)[:, HG * e : HG * e + HG, NOPE:DH, :]
            if how == "P":
                n = ROPE * PACK
                for i in range(2):
                    interleave_bank(grouped[:, 2 * n * i : 2 * n * i + 2 * n], [(n, src[:, 2 * i]), (n, src[:, 2 * i + 1])])
            else:
                interleave(how, grouped.rearrange("p (h f j) -> p h f j", f=ROPE, j=PACK), src)

        def wr_quant(half):
            base = 2 * HG * ROPE * half
            for lo, width in ((0, 512), (512, 256)):
                cols = slice(base + lo, base + lo + width)
                nc.vector.quantize_mx(out=wr_q[:, cols].bitcast(FP8X4), scales=wr_s[:, cols],
                                      in_=grp[("r", half)][:, PACK * lo : PACK * (lo + width)])

        cq, cs, xw, xt, xg, xq, xs, ct, cg = {}, {}, {}, {}, {}, {}, {}, {}, {}

        def widen(b, t):
            w = work.tile([P, E], BF16, name="xw", align_bytes=64)
            nc.vector.tensor_tensor(w[:], xb[(b, t // 2)][:, t % 2, :].bitcast(FP8), scale_bc[:], op=MULT)
            xw[(b, t)] = w

        def xpose(b, t):
            words = xw[(b, t)][:].bitcast(F32)
            for gh in range(2):
                bank = psum.tile([P, 2, 2, P], F32, name="xt")
                for e in range(2):
                    for u in range(2):
                        g = 2 * gh + e
                        nc.tensor.transpose(bank[:, e, u, :], words[:, 256 * g + u : 256 * (g + 1) : 2], ident[:])
                xt[(b, t, gh)] = bank

        def xexit(b, t):
            g4 = work.tile([P, GROUPS * P * PACK], BF16, name="xg", align_bytes=64)
            g_words = g4[:].bitcast(F32)
            for gh in range(2):
                nc.scalar.copy(g_words[:, 512 * gh : 512 * gh + 512].rearrange("p (g r u) -> p g r u", g=2, u=2),
                               xt[(b, t, gh)][:].rearrange("p g u r -> p g r u"))
            xg[(b, t)] = g4

        def x_quant(b, t):
            q = work.tile([P, GROUPS * P], U32, name="xq", align_bytes=64)
            s = work.tile([P, GROUPS * P], U8, name="xs", align_bytes=64)
            nc.vector.quantize_mx(out=q[:].bitcast(FP8X4), scales=s[:], in_=xg[(b, t)][:])
            xq[(b, t)] = q
            xs[(b, t)] = s

        def s1(b, t):
            bank = psum.tile([P, PACK, P], F32, name="ct")
            q, s = xq[(b, t)], xs[(b, t)]
            for j in range(PACK):
                for g in range(GROUPS):
                    nc.tensor.matmul_mx(
                        bank[:, j, :],
                        wd_q[:, g, P * j : P * j + P].bitcast(FP8X4), wd_s[:, g, P * j : P * j + P],
                        q[:, P * g : P * g + P].bitcast(FP8X4), s[:, P * g : P * g + P],
                        start=(g == 0), stop=(g == GROUPS - 1))
            ct[(b, t)] = bank

        def cexit(b, t):
            g4 = work.tile([P, P * PACK], BF16, name="cg", align_bytes=64)
            nc.scalar.copy(g4[:].rearrange("p (n j) -> p n j", j=PACK), ct[(b, t)][:].rearrange("p j n -> p n j"))
            cg[(b, t)] = g4

        def c_quant(b, t):
            q = keep.tile([P, P], U32, name="cq_%d_%d" % (b, t), align_bytes=64)
            s = keep.tile([P, P], U8, name="cs_%d_%d" % (b, t), align_bytes=64)
            nc.vector.quantize_mx(out=q[:].bitcast(FP8X4), scales=s[:], in_=cg[(b, t)][:])
            cq[(b, t)] = q
            cs[(b, t)] = s

        def up(ps, b, t, wq, ws, lo, n):
            nc.tensor.matmul_mx(ps, cq[(b, t)][:].bitcast(FP8X4), cs[(b, t)][:],
                                wq[:, lo : lo + n].bitcast(FP8X4), ws[:, lo : lo + n], start=True, stop=True)

        k_view = out_0.rearrange("b h (q t) f -> b q h (t f)", t=TILES)
        v_view = out_1.rearrange("b h (q t) f -> b q h (t f)", t=TILES)
        ov, ok, rp = {}, {}, {}

        def value(b, c, t):
            if t == 0:
                ov[(b, c)] = outs.tile([P, HG, TILES, DH], F32, name="ov", tag="o")
            o = ov[(b, c)]
            ps = psum.tile([P, HG, DH], F32, name="ps", tag="ps", bufs=4)
            up(ps[:].rearrange("p h f -> p (h f)"), b, t, wv_q, wv_s, 512 * c, 512)
            nc.scalar.copy(o[:, :, t, :], ps[:])
            if t == TILES - 1:
                nc.sync.dma_start(out=v_view[b, :, HG * c : HG * c + HG, :], in_=o[:].rearrange("p h t f -> p h (t f)"))

        def nope(b, c):
            ok[(b, c)] = outs.tile([P, HG, TILES, DH], F32, name="ok", tag="o")
            ps = psum.tile([P, TILES, HG, NOPE], F32, name="ps", tag="ps", bufs=4)
            for t in range(TILES):
                up(ps[:, t].rearrange("p h f -> p (h f)"), b, t, wn_q, wn_s, HG * NOPE * c, HG * NOPE)
            nc.scalar.copy(ok[(b, c)][:, :, :, 0:NOPE].rearrange("p h t f -> p t h f"), ps[:])

        def rope_mm(b, c, t):
            ps = psum.tile([P, HG * ROPE], F32, name="ps", tag="ps", bufs=4)
            up(ps[:, 0:256], b, t, wr_q, wr_s, HG * ROPE * c, 256)
            up(ps[:, 256:384], b, t, wr_q, wr_s, HG * ROPE * c + 256, 128)
            rp[(b, c, t)] = ps

        def rope_v(b, c, t):
            pairs = rp[(b, c, t)][:].rearrange("p (h i s) -> p h s i", h=HG, s=2)
            dst = ok[(b, c)][:, :, t, NOPE:DH].rearrange("p h (s i) -> p h s i", s=2)
            cos = trig[:, 1, t].unsqueeze(1).unsqueeze(1).to_broadcast([P, HG, 2, HALF])
            sin = sin_tab[:, t].unsqueeze(1).to_broadcast([P, HG, 2, HALF])
            cross = work.tile([P, HG, 2, HALF], F32, name="cross")
            nc.vector.tensor_tensor(cross[:], pairs[:, :, ::-1, :], sin, op=MULT)
            nc.vector.tensor_tensor(dst, pairs, cos, op=MULT)
            nc.gpsimd.tensor_tensor(dst, dst, cross[:], op=ADD)

        def k_store(b, c):
            nc.sync.dma_start(out=k_view[b, :, HG * c : HG * c + HG, :], in_=ok[(b, c)][:].rearrange("p h t f -> p h (t f)"))

        for g in range(GROUPS):
            wd_int(g, "VPPP"[g])
            wd_quant(g)
        def front(b, t):
            widen(b, t)
            xpose(b, t)
            xexit(b, t)
            x_quant(b, t)
            s1(b, t)
            cexit(b, t)
            c_quant(b, t)
        for t in range(TILES):
            front(0, t)
            wv_int(t, "P")
            wv_quant(t)
        tables()
        for c in range(2):
            wr_int(c, "P")
        wr_quant(0)
        wn_int("P")
        wn_quant()
        for c in range(NHG):
            for t in range(TILES):
                value(0, c, t)
            front(1, c)
            if c == 1:
                for e in range(2):
                    wr_int(2 + e, "S")
                wr_quant(1)
            if c < 2:
                nope(0, c)
                for t in range(TILES):
                    rope_mm(0, c, t)
                    rope_v(0, c, t)
                k_store(0, c)
        for j in range(2, 8):
            b, c = j // 4, j % 4
            nope(b, c)
            for t in range(TILES):
                rope_mm(b, c, t)
                rope_v(b, c, t)
                n = 4 * (j - 2) + t
                if n < 16:
                    value(1, n // 4, n % 4)
            k_store(b, c)
